import numpy as np
import ml_dtypes


def mxq(x, axis, fmt="e4m3"):
    dtype, down = {"e4m3": (ml_dtypes.float8_e4m3fn, 7), "e5m2": (ml_dtypes.float8_e5m2, 14)}[fmt]
    v = np.moveaxis(np.asarray(x, np.float32).astype(ml_dtypes.bfloat16).astype(np.float64), axis, -1)
    blocks = v.reshape(v.shape[:-1] + (-1, 32))
    amax = np.abs(blocks).max(-1, keepdims=True)
    byte = np.maximum(np.where(amax > 0, np.frexp(amax)[1] - 1 + 127, 0) - down, 1)
    scale = np.exp2(byte - 127.0)
    codes = (blocks / scale).astype(np.float32).astype(dtype).astype(np.float64)
    return np.moveaxis((codes * scale).reshape(v.shape), -1, axis)


WIDE = False


def mx_kscale(k):
    if not WIDE:
        return np.ones(k)
    levels = np.array([10, -10, 5, -5, 0])
    if k % 512:
        return np.exp2(np.random.permutation(np.resize(levels, k // 32))).repeat(32)
    a = np.empty((k // 512, 16))
    for p in range(k // 512):
        a[p, :8] = np.random.permutation(np.resize(levels, 8))
        for g in range(8):
            far = levels[np.abs(levels - a[p, g]) >= 10]
            a[p, g + 8] = far[np.random.randint(len(far))]
    return np.exp2(a.ravel()).repeat(32)


BF16 = ml_dtypes.bfloat16


def bf(x):
    return np.asarray(x, np.float32).astype(BF16)


def f64(x):
    return np.asarray(x).astype(np.float64)


B, S, D, N = 128, 32, 1024, 1024
EPS = 1e-5


def batch_bn(x, g, b):
    m = x.mean(axis=0)
    v = x.var(axis=0)
    return g * (x - m) / np.sqrt(v + EPS) + b


def setup_inputs():
    t, u = mx_kscale(D), mx_kscale(D)
    return {"s_z2": bf(np.random.standard_normal((B, S, D)) * 0.6 + np.random.standard_normal(D) * 0.4),
            "c_z2": bf(np.random.standard_normal((B, D)) * 0.6 + np.random.standard_normal(D) * 0.4),
            "s_g2": bf((1.0 + 0.1 * np.random.standard_normal(D)) * t),
            "s_be2": bf(0.1 * np.random.standard_normal(D) * t),
            "s_w3": bf(np.random.standard_normal((N, D)) * np.sqrt(2.0 / D) / t[None, :]),
            "s_b3": bf(0.1 * np.random.standard_normal(N)),
            "c_g2": bf((1.0 + 0.1 * np.random.standard_normal(D)) * u),
            "c_be2": bf(0.1 * np.random.standard_normal(D) * u),
            "c_w3": bf(np.random.standard_normal((N, D)) * np.sqrt(2.0 / D) / u[None, :]),
            "c_b3": bf(0.1 * np.random.standard_normal(N))}


def reference(s_z2, c_z2, s_g2, s_be2, s_w3, s_b3, c_g2, c_be2, c_w3, c_b3):
    c_h = np.maximum(batch_bn(f64(c_z2), f64(c_g2), f64(c_be2)), 0.0)
    c_out = (mxq(c_h, 1, "e4m3") @ mxq(f64(c_w3), 1, "e4m3").T) + f64(c_b3)
    s_h = np.maximum(batch_bn(f64(s_z2), f64(s_g2), f64(s_be2)), 0.0)
    s_p = (mxq(s_h, 2, "e4m3") @ mxq(f64(s_w3), 1, "e4m3").T) + f64(s_b3)
    s_out = s_p * c_out[:, None, :]
    aggregated_c = s_out.max(axis=1)
    return (s_out, aggregated_c)

@@ -1,0 +1,387 @@
+from contextlib import ExitStack
+
+import concourse.mybir as mybir
+from concourse.masks import make_identity
+
+F32 = mybir.dt.float32
+BF16 = mybir.dt.bfloat16
+U32 = mybir.dt.uint32
+U8 = mybir.dt.uint8
+FP8X4 = mybir.dt.float8_e4m3fn_x4
+ACT = mybir.ActivationFunctionType
+ALU = mybir.AluOpType
+
+P = 128
+SLICES = 32
+FEATURES = 1024
+OUTPUTS = 1024
+EPS = 1e-5
+PACK = 4
+PASSES = FEATURES // (P * PACK)
+QUARTERS = FEATURES // (2 * P)
+PER_PARTITION = FEATURES // P
+N_TILE = 512
+HALVES = OUTPUTS // N_TILE
+PAIR = 2
+PAIRS = SLICES // PAIR
+CONTEXT = -1
+CHUNK = 4
+
+FLOPS = 2 * (SLICES + 1) * P * FEATURES * OUTPUTS
+
+
+def tile_cgblock_pb_kernel(
+    tc, s_z2, c_z2, s_g2, s_be2, s_w3, s_b3, c_g2, c_be2, c_w3, c_b3, out_0, out_1
+):
+    nc = tc.nc
+    with ExitStack() as ctx:
+        consts = ctx.enter_context(tc.tile_pool(name="consts", bufs=1))
+        inputs = ctx.enter_context(tc.tile_pool(name="inputs", bufs=1))
+        weights = ctx.enter_context(tc.tile_pool(name="weights", bufs=1))
+        stage = ctx.enter_context(tc.tile_pool(name="stage", bufs=2))
+        stats = ctx.enter_context(tc.tile_pool(name="stats", bufs=3))
+        quantised = ctx.enter_context(tc.tile_pool(name="quantised", bufs=4))
+        results = ctx.enter_context(tc.tile_pool(name="results", bufs=3))
+        turned = ctx.enter_context(tc.psum_pool(name="turned", bufs=4))
+        sums = ctx.enter_context(tc.psum_pool(name="sums", bufs=1))
+        products = ctx.enter_context(tc.psum_pool(name="products", bufs=3))
+
+        identity = consts.tile([P, P], F32, name="identity")
+        make_identity(nc, identity[:])
+        minus_inv_batch = consts.tile([P, 1], BF16, name="minus_inv_batch")
+        nc.vector.memset(minus_inv_batch[:], -1.0 / P)
+        eps = consts.tile([P, 1], F32, name="eps")
+        nc.vector.memset(eps[:], EPS)
+        warm = consts.tile([P, 1], F32, name="warm")
+        nc.scalar.activation(out=warm[:], in_=eps[:], func=ACT.Sqrt)
+
+        vector_rows = consts.tile([P, 2 * P], F32, name="vector_rows")
+        nc.vector.memset(vector_rows[:], 0.0)
+        for v, vector in enumerate((s_g2, s_be2, c_g2, c_be2)):
+            nc.sync.dma_start(
+                out=vector_rows[:].bitcast(BF16)[PASSES * v : PASSES * (v + 1), :],
+                in_=vector.rearrange("(g w) -> g w", g=PASSES),
+            )
+
+        def load_slices(chunk):
+            rows = inputs.tile([P, CHUNK, FEATURES], BF16, name="s_rows%d" % chunk)
+            nc.sync.dma_start(out=rows[:], in_=s_z2[:, chunk * CHUNK : (chunk + 1) * CHUNK, :])
+            return rows
+
+        def load_weight(w, label):
+            halves = []
+            for half in range(HALVES):
+                rows = inputs.tile([P, N_TILE // P, FEATURES], BF16, name="%s%d" % (label, half))
+                nc.sync.dma_start(
+                    out=rows[:],
+                    in_=w[half * N_TILE : (half + 1) * N_TILE, :].rearrange("(c p) k -> p c k", p=P),
+                )
+                halves.append(rows)
+            return halves
+
+        def load_bias(b, label):
+            rows = consts.tile([P, OUTPUTS], BF16, name=label)
+            nc.sync.dma_start(out=rows[:], in_=b.partition_broadcast(P))
+            return rows
+
+        c_rows = inputs.tile([P, FEATURES], BF16, name="c_rows")
+        nc.sync.dma_start(out=c_rows[:], in_=c_z2)
+        s_rows = [load_slices(0)]
+        c_w_rows = load_weight(c_w3, "c_w_rows")
+        c_bias_rows = load_bias(c_b3, "c_bias_rows")
+        s_w_rows = load_weight(s_w3, "s_w_rows")
+        s_bias_rows = load_bias(s_b3, "s_bias_rows")
+        for chunk in range(1, SLICES // CHUNK):
+            s_rows.append(load_slices(chunk))
+
+        tables_ps = turned.tile([P, QUARTERS, P], F32, tag="turned", name="tables_ps")
+        tables = consts.tile([P, 4, PER_PARTITION], F32, name="tables")
+        spread_tables = tables[:].rearrange("p v (g u e) -> p u (v g) e", g=PASSES, u=2)
+        for u in range(2):
+            nc.tensor.transpose(tables_ps[:, u, :], vector_rows[:, u : 2 * P : 2], identity[:])
+            nc.vector.tensor_copy(
+                out=spread_tables[:, u, :, :],
+                in_=tables_ps[:, u, 0 : 4 * PASSES].bitcast(BF16).rearrange("p (r e) -> p r e", e=2),
+            )
+        s_gain, s_shift = tables[:, 0, :], tables[:, 1, :]
+        c_gain, c_shift = tables[:, 2, :], tables[:, 3, :]
+
+        def every_second(words, q):
+            first = (q // 2) * 2 * P + q % 2
+            return words[:, first : (q // 2 + 1) * 2 * P : 2]
+
+        def halves_of(xt):
+            return xt[:].bitcast(BF16).rearrange("p q (b e) -> p q e b", e=2)
+
+        def blocks_of(group):
+            if group == CONTEXT:
+                return [c_rows[:]]
+            first = group * PAIR
+            return [s_rows[(first + s) // CHUNK][:, (first + s) % CHUNK, :] for s in range(PAIR)]
+
+        def size_of(group):
+            return len(blocks_of(group)) if CONTEXT <= group < PAIRS else 0
+
+        xts, mean_ps, neg_mean, std = {}, {}, {}, {}
+        scale, bias, hidden, grouped, codes, planes = {}, {}, {}, {}, {}, {}
+
+        def turn(group, s):
+            rows = blocks_of(group)[s]
+            if s == 0:
+                xts[group] = []
+                mean_ps[group] = sums.tile(
+                    [P, size_of(group), PER_PARTITION], F32, tag="mean_ps", name="mean_ps"
+                )
+            words = rows.bitcast(F32)
+            xt = turned.tile([P, QUARTERS, P], F32, tag="turned", name="xt")
+            for q in range(QUARTERS):
+                nc.tensor.transpose(xt[:, q, :], every_second(words, q), identity[:])
+            xts[group].append(xt)
+            by_place = rows.rearrange("b (g p t) -> b g t p", g=PASSES, t=PACK)
+            for j in range(PER_PARTITION):
+                nc.tensor.matmul(
+                    mean_ps[group][:, s, j : j + 1],
+                    lhsT=by_place[:, j // PACK, j % PACK, :],
+                    rhs=minus_inv_batch[:],
+                    start=True,
+                    stop=True,
+                )
+
+        def spread(group):
+            shape = [P, size_of(group), PER_PARTITION]
+            neg_mean[group] = stats.tile(shape, F32, tag="neg_mean", name="neg_mean")
+            sq_sum = stats.tile(shape, F32, tag="sq_sum", name="sq_sum")
+            for s, xt in enumerate(xts[group]):
+                nc.scalar.copy(out=neg_mean[group][:, s, :], in_=mean_ps[group][:, s, :])
+                squares = stage.tile([P, PER_PARTITION, P], BF16, tag="squares", name="squares")
+                for q in range(QUARTERS):
+                    for e in range(2):
+                        j = 2 * q + e
+                        nc.scalar.activation(
+                            out=squares[:, j, :],
+                            in_=halves_of(xt)[:, q, e, :],
+                            func=ACT.Square,
+                            bias=neg_mean[group][:, s, j : j + 1],
+                            scale=1.0,
+                            accum_out=sq_sum[:, s, j : j + 1],
+                        )
+            std[group] = stats.tile(shape, F32, tag="std", name="std")
+            nc.scalar.activation(
+                out=std[group][:], in_=sq_sum[:], func=ACT.Sqrt, bias=eps[:], scale=1.0 / P
+            )
+
+        def coefficient_steps(group):
+            shape = [P, size_of(group), PER_PARTITION]
+            gain, shift = (c_gain, c_shift) if group == CONTEXT else (s_gain, s_shift)
+            inv_std = stats.tile(shape, F32, tag="inv_std", name="inv_std")
+            centre = stats.tile(shape, F32, tag="centre", name="centre")
+            scale[group] = stats.tile(shape, F32, tag="scale", name="scale")
+            bias[group] = stats.tile(shape, F32, tag="bias", name="bias")
+            return [
+                lambda: nc.vector.reciprocal(out=inv_std[:], in_=std[group][:]),
+                lambda: nc.vector.tensor_tensor(
+                    out=scale[group][:],
+                    in0=inv_std[:],
+                    in1=gain.unsqueeze(1).to_broadcast(shape),
+                    op=ALU.mult,
+                ),
+                lambda: nc.vector.tensor_tensor(
+                    out=centre[:], in0=neg_mean[group][:], in1=scale[group][:], op=ALU.mult
+                ),
+                lambda: nc.vector.tensor_tensor(
+                    out=bias[group][:],
+                    in0=centre[:],
+                    in1=shift.unsqueeze(1).to_broadcast(shape),
+                    op=ALU.add,
+                ),
+            ]
+
+        def activate(group, s):
+            if s == 0:
+                width = size_of(group) * PASSES * P
+                hidden[group] = stage.tile([P, PACK, width], BF16, tag="hidden", name="hidden")
+            for q in range(QUARTERS):
+                for e in range(2):
+                    j = 2 * q + e
+                    g, t = j // PACK, j % PACK
+                    first = (s * PASSES + g) * P
+                    nc.scalar.activation(
+                        out=hidden[group][:, t, first : first + P],
+                        in_=halves_of(xts[group][s])[:, q, e, :],
+                        func=ACT.Relu,
+                        bias=bias[group][:, s, j : j + 1],
+                        scale=scale[group][:, s, j : j + 1],
+                    )
+
+        def regroup_second_half(group):
+            width = size_of(group) * PASSES * P
+            middle = width // 2
+            grouped[group] = stage.tile(
+                [P, width, PACK], BF16, tag="grouped", name="grouped", align_bytes=64
+            )
+            nc.scalar.copy(
+                out=grouped[group][:, middle:, :].rearrange("p (c i) t -> p c t i", i=4),
+                in_=hidden[group][:, :, middle:].rearrange("p t (c i) -> p c t i", i=4),
+            )
+
+        def regroup_first_half(group):
+            middle = size_of(group) * PASSES * P // 2
+            nc.vector.tensor_copy(
+                out=grouped[group][:, :middle, :].rearrange("p (c i) t -> p c t i", i=4),
+                in_=hidden[group][:, :, :middle].rearrange("p t (c i) -> p c t i", i=4),
+            )
+
+        def quantise(group):
+            width = size_of(group) * PASSES * P
+            codes[group] = quantised.tile([P, width], U32, tag="codes", name="codes", align_bytes=64)
+            planes[group] = quantised.tile([P, width], U8, tag="planes", name="planes", align_bytes=64)
+            nc.vector.quantize_mx(
+                out=codes[group][:].bitcast(FP8X4),
+                scales=planes[group][:],
+                in_=grouped[group][:].rearrange("p w t -> p (w t)"),
+            )
+
+        def weight_tiles(label):
+            w_codes = weights.tile([P, PASSES, OUTPUTS], U32, name=label + "_codes", align_bytes=64)
+            w_planes = weights.tile([P, PASSES, OUTPUTS], U8, name=label + "_planes", align_bytes=64)
+            return w_codes, w_planes
+
+        def quantise_weight_half(w_rows, w_codes, w_planes, half):
+            words = w_rows[half][:].bitcast(F32)
+            cols = slice(half * N_TILE, (half + 1) * N_TILE)
+            for g in range(PASSES):
+                grouped = stage.tile(
+                    [P, N_TILE, PACK], BF16, tag="w_grouped", name="w_grouped", align_bytes=64
+                )
+                grouped_words = grouped[:].bitcast(F32)
+                for bank in range(2):
+                    wt = products.tile([P, 2, 2 * P], F32, tag="acc", name="wt")
+                    for u in range(2):
+                        q = 2 * g + u
+                        for c in range(2):
+                            nc.tensor.transpose(
+                                wt[:, u, c * P : (c + 1) * P],
+                                every_second(words[:, 2 * bank + c, :], q),
+                                identity[:],
+                            )
+                    target = grouped_words[:, bank * 2 * P : (bank + 1) * 2 * P, :]
+                    if bank == 0:
+                        nc.vector.tensor_copy(out=target, in_=wt[:].rearrange("p u n -> p n u"))
+                    else:
+                        nc.scalar.copy(out=target, in_=wt[:].rearrange("p u n -> p n u"))
+                nc.vector.quantize_mx(
+                    out=w_codes[:, g, cols].bitcast(FP8X4),
+                    scales=w_planes[:, g, cols],
+                    in_=grouped[:].rearrange("p n t -> p (n t)"),
+                )
+
+        def project(group, s, w_codes, w_planes, half):
+            acc = products.tile([P, N_TILE], F32, tag="acc", name="acc")
+            cols = slice(half * N_TILE, (half + 1) * N_TILE)
+            for g in range(PASSES):
+                rows = slice((s * PASSES + g) * P, (s * PASSES + g + 1) * P)
+                nc.tensor.matmul_mx(
+                    out=acc[:],
+                    lhsT=codes[group][:, rows].bitcast(FP8X4),
+                    lhsT_scale=planes[group][:, rows],
+                    rhs=w_codes[:, g, cols].bitcast(FP8X4),
+                    rhs_scale=w_planes[:, g, cols],
+                    start=(g == 0),
+                    stop=(g == PASSES - 1),
+                )
+            return acc
+
+        c_w_codes, c_w_planes = weight_tiles("c_w")
+        s_w_codes, s_w_planes = weight_tiles("s_w")
+
+        gate = consts.tile([P, OUTPUTS], F32, name="gate")
+        gated_bias = consts.tile([P, OUTPUTS], F32, name="gated_bias")
+        best = consts.tile([P, PAIR, OUTPUTS], F32, name="best")
+        gated = {}
+
+        def open_gate():
+            for half in range(HALVES):
+                cols = slice(half * N_TILE, (half + 1) * N_TILE)
+                acc = project(CONTEXT, 0, c_w_codes, c_w_planes, half)
+                nc.vector.tensor_tensor(
+                    out=gate[:, cols], in0=acc[:], in1=c_bias_rows[:, cols], op=ALU.add
+                )
+                nc.vector.tensor_tensor(
+                    out=gated_bias[:, cols], in0=gate[:, cols], in1=s_bias_rows[:, cols], op=ALU.mult
+                )
+
+        def multiply(pair):
+            if pair == 0:
+                gated[pair] = best
+            else:
+                gated[pair] = results.tile([P, PAIR, OUTPUTS], F32, tag="gated", name="gated")
+            for s in range(PAIR):
+                for half in range(HALVES):
+                    cols = slice(half * N_TILE, (half + 1) * N_TILE)
+                    acc = project(pair, s, s_w_codes, s_w_planes, half)
+                    nc.vector.tensor_tensor(
+                        out=gated[pair][:, s, cols], in0=acc[:], in1=gate[:, cols], op=ALU.mult
+                    )
+
+        def add_bias_and_store(pair, s):
+            biased = results.tile([P, OUTPUTS], F32, tag="biased", name="biased")
+            nc.vector.tensor_tensor(
+                out=biased[:], in0=gated[pair][:, s, :], in1=gated_bias[:], op=ALU.add
+            )
+            nc.sync.dma_start(out=out_0[:, pair * PAIR + s, :], in_=biased[:])
+
+        def pool(pair, s):
+            if pair > 0:
+                nc.vector.tensor_tensor(
+                    out=best[:, s, :], in0=best[:, s, :], in1=gated[pair][:, s, :], op=ALU.max
+                )
+
+        def step(n):
+            if n == CONTEXT:
+                open_gate()
+            if n >= 0:
+                multiply(n)
+            if size_of(n + 2):
+                spread(n + 2)
+            for s in range(PAIR):
+                if s < size_of(n + 1):
+                    activate(n + 1, s)
+                if s < size_of(n + 3):
+                    turn(n + 3, s)
+            if size_of(n + 1):
+                regroup_second_half(n + 1)
+            long_steps = []
+            if n >= 0:
+                long_steps.append(lambda: add_bias_and_store(n, 0))
+            if size_of(n + 1):
+                long_steps.append(lambda: regroup_first_half(n + 1))
+            if n >= 0:
+                long_steps.append(lambda: add_bias_and_store(n, 1))
+            if size_of(n + 1):
+                long_steps.append(lambda: quantise(n + 1))
+            if n >= 0:
+                long_steps.append(lambda: pool(n, 0))
+                long_steps.append(lambda: pool(n, 1))
+            short_steps = coefficient_steps(n + 2) if size_of(n + 2) else []
+            for k in range(max(len(long_steps), len(short_steps))):
+                if k < len(long_steps):
+                    long_steps[k]()
+                if k < len(short_steps):
+                    short_steps[k]()
+
+        step(CONTEXT - 3)
+        step(CONTEXT - 2)
+        for half in range(HALVES):
+            quantise_weight_half(c_w_rows, c_w_codes, c_w_planes, half)
+        step(CONTEXT - 1)
+        for half in range(HALVES):
+            quantise_weight_half(s_w_rows, s_w_codes, s_w_planes, half)
+        step(CONTEXT)
+        with tc.manual_schedule():
+            for n in range(PAIRS):
+                step(n)
+
+        pooled = results.tile([P, OUTPUTS], F32, tag="biased", name="pooled")
+        nc.vector.tensor_tensor(out=pooled[:], in0=best[:, 0, :], in1=best[:, 1, :], op=ALU.max)
+        nc.vector.tensor_tensor(out=pooled[:], in0=pooled[:], in1=gated_bias[:], op=ALU.add)
+        nc.sync.dma_start(out=out_1, in_=pooled[:])

@@ -213,9 +213,9 @@ def tile_cgblock_pb_kernel(
                         scale=scale[group][:, s, j : j + 1],
                     )
 
-        def regroup_second_half(group):
+        def regroup_last_columns(group):
             width = size_of(group) * PASSES * P
-            middle = width // 2
+            middle = 3 * width // 4
             grouped[group] = stage.tile(
                 [P, width, PACK], BF16, tag="grouped", name="grouped", align_bytes=64
             )
@@ -224,8 +224,8 @@ def tile_cgblock_pb_kernel(
                 in_=hidden[group][:, :, middle:].rearrange("p t (c i) -> p c t i", i=4),
             )
 
-        def regroup_first_half(group):
-            middle = size_of(group) * PASSES * P // 2
+        def regroup_first_columns(group):
+            middle = 3 * size_of(group) * PASSES * P // 4
             nc.vector.tensor_copy(
                 out=grouped[group][:, :middle, :].rearrange("p (c i) t -> p c t i", i=4),
                 in_=hidden[group][:, :, :middle].rearrange("p t (c i) -> p c t i", i=4),
@@ -330,6 +330,14 @@ def tile_cgblock_pb_kernel(
             )
             nc.sync.dma_start(out=out_0[:, pair * PAIR + s, :], in_=biased[:])
 
+        def on_gpsimd(pair, s):
+            return s == 1 and 0 < pair < PAIRS - 1
+
+        def add_bias_in_place_and_store(pair, s):
+            product = gated[pair][:, s, :]
+            nc.gpsimd.tensor_tensor(out=product, in0=product, in1=gated_bias[:], op=ALU.add)
+            nc.sync.dma_start(out=out_0[:, pair * PAIR + s, :], in_=product)
+
         def pool(pair, s):
             if pair > 0:
                 nc.vector.tensor_tensor(
@@ -349,13 +357,13 @@ def tile_cgblock_pb_kernel(
                 if s < size_of(n + 3):
                     turn(n + 3, s)
             if size_of(n + 1):
-                regroup_second_half(n + 1)
+                regroup_last_columns(n + 1)
             long_steps = []
             if n >= 0:
                 long_steps.append(lambda: add_bias_and_store(n, 0))
             if size_of(n + 1):
-                long_steps.append(lambda: regroup_first_half(n + 1))
-            if n >= 0:
+                long_steps.append(lambda: regroup_first_columns(n + 1))
+            if n >= 0 and not on_gpsimd(n, 1):
                 long_steps.append(lambda: add_bias_and_store(n, 1))
             if size_of(n + 1):
                 long_steps.append(lambda: quantise(n + 1))
@@ -368,6 +376,8 @@ def tile_cgblock_pb_kernel(
                     long_steps[k]()
                 if k < len(short_steps):
                     short_steps[k]()
+            if on_gpsimd(n, 1):
+                add_bias_in_place_and_store(n, 1)
 
         step(CONTEXT - 3)
         step(CONTEXT - 2)

@@ -26,6 +26,7 @@ PAIR = 2
 PAIRS = SLICES // PAIR
 CONTEXT = -1
 CHUNK = 4
+SPLIT = N_TILE
 
 FLOPS = 2 * (SLICES + 1) * P * FEATURES * OUTPUTS
 
@@ -43,7 +44,7 @@ def tile_cgblock_pb_kernel(
         quantised = ctx.enter_context(tc.tile_pool(name="quantised", bufs=4))
         results = ctx.enter_context(tc.tile_pool(name="results", bufs=3))
         turned = ctx.enter_context(tc.psum_pool(name="turned", bufs=4))
-        sums = ctx.enter_context(tc.psum_pool(name="sums", bufs=1))
+        kept = ctx.enter_context(tc.psum_pool(name="kept", bufs=1))
         products = ctx.enter_context(tc.psum_pool(name="products", bufs=3))
 
         identity = consts.tile([P, P], F32, name="identity")
@@ -129,8 +130,8 @@ def tile_cgblock_pb_kernel(
             rows = blocks_of(group)[s]
             if s == 0:
                 xts[group] = []
-                mean_ps[group] = sums.tile(
-                    [P, size_of(group), PER_PARTITION], F32, tag="mean_ps", name="mean_ps"
+                mean_ps[group] = products.tile(
+                    [P, size_of(group), PER_PARTITION], F32, tag="acc", name="mean_ps"
                 )
             words = rows.bitcast(F32)
             xt = turned.tile([P, QUARTERS, P], F32, tag="turned", name="xt")
@@ -147,12 +148,15 @@ def tile_cgblock_pb_kernel(
                     stop=True,
                 )
 
-        def spread(group):
+        def take_means(group):
             shape = [P, size_of(group), PER_PARTITION]
             neg_mean[group] = stats.tile(shape, F32, tag="neg_mean", name="neg_mean")
+            nc.scalar.copy(out=neg_mean[group][:], in_=mean_ps[group][:])
+
+        def spread(group):
+            shape = [P, size_of(group), PER_PARTITION]
             sq_sum = stats.tile(shape, F32, tag="sq_sum", name="sq_sum")
             for s, xt in enumerate(xts[group]):
-                nc.scalar.copy(out=neg_mean[group][:, s, :], in_=mean_ps[group][:, s, :])
                 squares = stage.tile([P, PER_PARTITION, P], BF16, tag="squares", name="squares")
                 for q in range(QUARTERS):
                     for e in range(2):
@@ -297,6 +301,7 @@ def tile_cgblock_pb_kernel(
         gate = consts.tile([P, OUTPUTS], F32, name="gate")
         gated_bias = consts.tile([P, OUTPUTS], F32, name="gated_bias")
         best = consts.tile([P, PAIR, OUTPUTS], F32, name="best")
+        gated_bias_ps = kept.tile([P, OUTPUTS - SPLIT], F32, name="gated_bias_ps")
         gated = {}
 
         def open_gate():
@@ -309,6 +314,9 @@ def tile_cgblock_pb_kernel(
                 nc.vector.tensor_tensor(
                     out=gated_bias[:, cols], in0=gate[:, cols], in1=s_bias_rows[:, cols], op=ALU.mult
                 )
+            nc.tensor.matmul(
+                gated_bias_ps[:], lhsT=identity[:], rhs=gated_bias[:, SPLIT:], start=True, stop=True
+            )
 
         def multiply(pair):
             if pair == 0:
@@ -323,20 +331,38 @@ def tile_cgblock_pb_kernel(
                         out=gated[pair][:, s, cols], in0=acc[:], in1=gate[:, cols], op=ALU.mult
                     )
 
-        def add_bias_and_store(pair, s):
-            biased = results.tile([P, OUTPUTS], F32, tag="biased", name="biased")
+        def add_bias_and_store(pair):
+            slices = slice(pair * PAIR, (pair + 1) * PAIR)
+            first = SPLIT if on_gpsimd(pair) else 0
+            biased = results.tile([P, PAIR, OUTPUTS - first], F32, tag="biased", name="biased")
             nc.vector.tensor_tensor(
-                out=biased[:], in0=gated[pair][:, s, :], in1=gated_bias[:], op=ALU.add
+                out=biased[:, :, SPLIT - first :],
+                in0=gated[pair][:, :, SPLIT:],
+                in1=gated_bias_ps[:].unsqueeze(1).to_broadcast([P, PAIR, OUTPUTS - SPLIT]),
+                op=ALU.add,
             )
-            nc.sync.dma_start(out=out_0[:, pair * PAIR + s, :], in_=biased[:])
+            if first == 0:
+                nc.vector.tensor_tensor(
+                    out=biased[:, :, :SPLIT],
+                    in0=gated[pair][:, :, :SPLIT],
+                    in1=gated_bias[:, :SPLIT].unsqueeze(1).to_broadcast([P, PAIR, SPLIT]),
+                    op=ALU.add,
+                )
+            nc.sync.dma_start(out=out_0[:, slices, first:], in_=biased[:])
 
-        def on_gpsimd(pair, s):
-            return s == 1 and 0 < pair < PAIRS - 1
+        def on_gpsimd(pair):
+            return 0 < pair < PAIRS - 1
 
-        def add_bias_in_place_and_store(pair, s):
-            product = gated[pair][:, s, :]
-            nc.gpsimd.tensor_tensor(out=product, in0=product, in1=gated_bias[:], op=ALU.add)
-            nc.sync.dma_start(out=out_0[:, pair * PAIR + s, :], in_=product)
+        def add_bias_in_place_and_store(pair):
+            slices = slice(pair * PAIR, (pair + 1) * PAIR)
+            part = gated[pair][:, :, :SPLIT]
+            nc.gpsimd.tensor_tensor(
+                out=part,
+                in0=part,
+                in1=gated_bias[:, :SPLIT].unsqueeze(1).to_broadcast([P, PAIR, SPLIT]),
+                op=ALU.add,
+            )
+            nc.sync.dma_start(out=out_0[:, slices, :SPLIT], in_=part)
 
         def pool(pair, s):
             if pair > 0:
@@ -358,13 +384,13 @@ def tile_cgblock_pb_kernel(
                     turn(n + 3, s)
             if size_of(n + 1):
                 regroup_last_columns(n + 1)
+            if size_of(n + 3):
+                take_means(n + 3)
             long_steps = []
             if n >= 0:
-                long_steps.append(lambda: add_bias_and_store(n, 0))
+                long_steps.append(lambda: add_bias_and_store(n))
             if size_of(n + 1):
                 long_steps.append(lambda: regroup_first_columns(n + 1))
-            if n >= 0 and not on_gpsimd(n, 1):
-                long_steps.append(lambda: add_bias_and_store(n, 1))
             if size_of(n + 1):
                 long_steps.append(lambda: quantise(n + 1))
             if n >= 0:
@@ -376,8 +402,8 @@ def tile_cgblock_pb_kernel(
                     long_steps[k]()
                 if k < len(short_steps):
                     short_steps[k]()
-            if on_gpsimd(n, 1):
-                add_bias_in_place_and_store(n, 1)
+            if on_gpsimd(n):
+                add_bias_in_place_and_store(n)
 
         step(CONTEXT - 3)
         step(CONTEXT - 2)

@@ -314,6 +314,8 @@ def tile_cgblock_pb_kernel(
                 nc.vector.tensor_tensor(
                     out=gated_bias[:, cols], in0=gate[:, cols], in1=s_bias_rows[:, cols], op=ALU.mult
                 )
+
+        def keep_gated_bias():
             nc.tensor.matmul(
                 gated_bias_ps[:], lhsT=identity[:], rhs=gated_bias[:, SPLIT:], start=True, stop=True
             )
@@ -323,8 +325,8 @@ def tile_cgblock_pb_kernel(
                 gated[pair] = best
             else:
                 gated[pair] = results.tile([P, PAIR, OUTPUTS], F32, tag="gated", name="gated")
-            for s in range(PAIR):
-                for half in range(HALVES):
+            for half in reversed(range(HALVES)):
+                for s in range(PAIR):
                     cols = slice(half * N_TILE, (half + 1) * N_TILE)
                     acc = project(pair, s, s_w_codes, s_w_planes, half)
                     nc.vector.tensor_tensor(
@@ -333,21 +335,15 @@ def tile_cgblock_pb_kernel(
 
         def add_bias_and_store(pair):
             slices = slice(pair * PAIR, (pair + 1) * PAIR)
-            first = SPLIT if on_gpsimd(pair) else 0
-            biased = results.tile([P, PAIR, OUTPUTS - first], F32, tag="biased", name="biased")
+            first, source = (SPLIT, gated_bias_ps) if on_gpsimd(pair) else (0, gated_bias)
+            shape = [P, PAIR, OUTPUTS - first]
+            biased = results.tile(shape, F32, tag="biased", name="biased")
             nc.vector.tensor_tensor(
-                out=biased[:, :, SPLIT - first :],
-                in0=gated[pair][:, :, SPLIT:],
-                in1=gated_bias_ps[:].unsqueeze(1).to_broadcast([P, PAIR, OUTPUTS - SPLIT]),
+                out=biased[:],
+                in0=gated[pair][:, :, first:],
+                in1=source[:].unsqueeze(1).to_broadcast(shape),
                 op=ALU.add,
             )
-            if first == 0:
-                nc.vector.tensor_tensor(
-                    out=biased[:, :, :SPLIT],
-                    in0=gated[pair][:, :, :SPLIT],
-                    in1=gated_bias[:, :SPLIT].unsqueeze(1).to_broadcast([P, PAIR, SPLIT]),
-                    op=ALU.add,
-                )
             nc.sync.dma_start(out=out_0[:, slices, first:], in_=biased[:])
 
         def on_gpsimd(pair):
@@ -375,7 +371,10 @@ def tile_cgblock_pb_kernel(
                 open_gate()
             if n >= 0:
                 multiply(n)
+            if n == 0:
+                keep_gated_bias()
             if size_of(n + 2):
+                take_means(n + 2)
                 spread(n + 2)
             for s in range(PAIR):
                 if s < size_of(n + 1):
@@ -384,8 +383,6 @@ def tile_cgblock_pb_kernel(
                     turn(n + 3, s)
             if size_of(n + 1):
                 regroup_last_columns(n + 1)
-            if size_of(n + 3):
-                take_means(n + 3)
             long_steps = []
             if n >= 0:
                 long_steps.append(lambda: add_bias_and_store(n))

@@ -26,6 +26,8 @@ PAIR = 2
 PAIRS = SLICES // PAIR
 CONTEXT = -1
 CHUNK = 4
+POOLED_FIRST = 3 * OUTPUTS // 4
+BN_WORDS = 6
 SPLIT = N_TILE
 
 FLOPS = 2 * (SLICES + 1) * P * FEATURES * OUTPUTS
@@ -64,10 +66,14 @@ def tile_cgblock_pb_kernel(
                 in_=vector.rearrange("(g w) -> g w", g=PASSES),
             )
 
-        def load_slices(chunk):
-            rows = inputs.tile([P, CHUNK, FEATURES], BF16, name="s_rows%d" % chunk)
-            nc.sync.dma_start(out=rows[:], in_=s_z2[:, chunk * CHUNK : (chunk + 1) * CHUNK, :])
-            return rows
+        s_blocks = []
+
+        def load_slices(size):
+            first = len(s_blocks)
+            rows = inputs.tile([P, size, FEATURES], BF16, name="s_rows%d" % first)
+            nc.sync.dma_start(out=rows[:], in_=s_z2[:, first : first + size, :])
+            for s in range(size):
+                s_blocks.append(rows[:, s, :])
 
         def load_weight(w, label):
             halves = []
@@ -80,20 +86,36 @@ def tile_cgblock_pb_kernel(
                 halves.append(rows)
             return halves
 
-        def load_bias(b, label):
-            rows = consts.tile([P, OUTPUTS], BF16, name=label)
-            nc.sync.dma_start(out=rows[:], in_=b.partition_broadcast(P))
-            return rows
-
+        bias_rows = consts.tile([P, 2, OUTPUTS], BF16, name="bias_rows")
+        nc.gpsimd.memset(bias_rows[:], 0.0)
         c_rows = inputs.tile([P, FEATURES], BF16, name="c_rows")
         nc.sync.dma_start(out=c_rows[:], in_=c_z2)
-        s_rows = [load_slices(0)]
+        load_slices(PAIR)
         c_w_rows = load_weight(c_w3, "c_w_rows")
-        c_bias_rows = load_bias(c_b3, "c_bias_rows")
+        for v, vector in enumerate((c_b3, s_b3)):
+            nc.sync.dma_start(out=bias_rows[0:1, v, :], in_=vector.unsqueeze(0))
+        load_slices(PAIR)
         s_w_rows = load_weight(s_w3, "s_w_rows")
-        s_bias_rows = load_bias(s_b3, "s_bias_rows")
-        for chunk in range(1, SLICES // CHUNK):
-            s_rows.append(load_slices(chunk))
+        while len(s_blocks) < SLICES:
+            load_slices(CHUNK)
+        ones = consts.tile([P, P], BF16, name="ones")
+        nc.gpsimd.memset(ones[:], 1.0)
+        c_bias = consts.tile([P, OUTPUTS], F32, name="c_bias")
+
+        def spread_bias(v, cols):
+            spread_ps = kept.tile([P, N_TILE], F32, tag="kept", name="spread_ps")
+            nc.tensor.matmul(
+                spread_ps[:], lhsT=ones[:], rhs=bias_rows[:, v, cols], start=True, stop=True
+            )
+            return spread_ps
+
+        def half_columns(half):
+            return slice(half * N_TILE, (half + 1) * N_TILE)
+
+        def spread_context_bias():
+            for half in range(HALVES):
+                spread_ps = spread_bias(0, half_columns(half))
+                nc.scalar.copy(out=c_bias[:, half_columns(half)], in_=spread_ps[:])
 
         tables_ps = turned.tile([P, QUARTERS, P], F32, tag="turned", name="tables_ps")
         tables = consts.tile([P, 4, PER_PARTITION], F32, name="tables")
@@ -117,27 +139,32 @@ def tile_cgblock_pb_kernel(
         def blocks_of(group):
             if group == CONTEXT:
                 return [c_rows[:]]
-            first = group * PAIR
-            return [s_rows[(first + s) // CHUNK][:, (first + s) % CHUNK, :] for s in range(PAIR)]
+            return s_blocks[group * PAIR : (group + 1) * PAIR]
 
         def size_of(group):
             return len(blocks_of(group)) if CONTEXT <= group < PAIRS else 0
 
-        xts, mean_ps, neg_mean, std = {}, {}, {}, {}
+        def by_vector(group):
+            return group in (CONTEXT, 0)
+
+        xts, mean_ps, neg_mean, moments, std = {}, {}, {}, {}, {}
         scale, bias, hidden, grouped, codes, planes = {}, {}, {}, {}, {}, {}
 
         def turn(group, s):
             rows = blocks_of(group)[s]
             if s == 0:
                 xts[group] = []
-                mean_ps[group] = products.tile(
-                    [P, size_of(group), PER_PARTITION], F32, tag="acc", name="mean_ps"
-                )
+                if not by_vector(group):
+                    mean_ps[group] = products.tile(
+                        [P, size_of(group), PER_PARTITION], F32, tag="acc", name="mean_ps"
+                    )
             words = rows.bitcast(F32)
             xt = turned.tile([P, QUARTERS, P], F32, tag="turned", name="xt")
             for q in range(QUARTERS):
                 nc.tensor.transpose(xt[:, q, :], every_second(words, q), identity[:])
             xts[group].append(xt)
+            if by_vector(group):
+                return
             by_place = rows.rearrange("b (g p t) -> b g t p", g=PASSES, t=PACK)
             for j in range(PER_PARTITION):
                 nc.tensor.matmul(
@@ -152,6 +179,28 @@ def tile_cgblock_pb_kernel(
             shape = [P, size_of(group), PER_PARTITION]
             neg_mean[group] = stats.tile(shape, F32, tag="neg_mean", name="neg_mean")
             nc.scalar.copy(out=neg_mean[group][:], in_=mean_ps[group][:])
+
+        def measure(group):
+            shape = [P, size_of(group), QUARTERS, BN_WORDS]
+            moments[group] = stats.tile(shape, F32, tag="moments", name="moments")
+            for s, xt in enumerate(xts[group]):
+                for q in range(QUARTERS):
+                    nc.vector.bn_stats(
+                        out=moments[group][:, s, q, :], in_=xt[:, q, :].bitcast(BF16)
+                    )
+            std[group] = stats.tile(
+                [P, size_of(group), PER_PARTITION], F32, tag="std", name="std"
+            )
+            nc.scalar.activation(
+                out=by_q(std[group]),
+                in_=moments[group][:, :, :, 2:BN_WORDS:3],
+                func=ACT.Sqrt,
+                bias=eps[:],
+                scale=1.0 / P,
+            )
+
+        def by_q(tile):
+            return tile[:].rearrange("p s (q e) -> p s q e", e=2)
 
         def spread(group):
             shape = [P, size_of(group), PER_PARTITION]
@@ -181,6 +230,10 @@ def tile_cgblock_pb_kernel(
             centre = stats.tile(shape, F32, tag="centre", name="centre")
             scale[group] = stats.tile(shape, F32, tag="scale", name="scale")
             bias[group] = stats.tile(shape, F32, tag="bias", name="bias")
+            if by_vector(group):
+                means, sign = moments[group][:, :, :, 1:BN_WORDS:3], ALU.subtract
+            else:
+                means, sign = by_q(neg_mean[group]), ALU.add
             return [
                 lambda: nc.vector.reciprocal(out=inv_std[:], in_=std[group][:]),
                 lambda: nc.vector.tensor_tensor(
@@ -190,13 +243,13 @@ def tile_cgblock_pb_kernel(
                     op=ALU.mult,
                 ),
                 lambda: nc.vector.tensor_tensor(
-                    out=centre[:], in0=neg_mean[group][:], in1=scale[group][:], op=ALU.mult
+                    out=by_q(centre), in0=means, in1=by_q(scale[group]), op=ALU.mult
                 ),
                 lambda: nc.vector.tensor_tensor(
                     out=bias[group][:],
-                    in0=centre[:],
-                    in1=shift.unsqueeze(1).to_broadcast(shape),
-                    op=ALU.add,
+                    in0=shift.unsqueeze(1).to_broadcast(shape),
+                    in1=centre[:],
+                    op=sign,
                 ),
             ]
 
@@ -217,9 +270,13 @@ def tile_cgblock_pb_kernel(
                         scale=scale[group][:, s, j : j + 1],
                     )
 
+        def scalar_columns(group):
+            width = size_of(group) * PASSES * P
+            return 0 if group == PAIRS - 1 else 3 * width // 4
+
         def regroup_last_columns(group):
             width = size_of(group) * PASSES * P
-            middle = 3 * width // 4
+            middle = scalar_columns(group)
             grouped[group] = stage.tile(
                 [P, width, PACK], BF16, tag="grouped", name="grouped", align_bytes=64
             )
@@ -229,7 +286,7 @@ def tile_cgblock_pb_kernel(
             )
 
         def regroup_first_columns(group):
-            middle = 3 * size_of(group) * PASSES * P // 4
+            middle = scalar_columns(group)
             nc.vector.tensor_copy(
                 out=grouped[group][:, :middle, :].rearrange("p (c i) t -> p c t i", i=4),
                 in_=hidden[group][:, :, :middle].rearrange("p t (c i) -> p c t i", i=4),
@@ -269,7 +326,7 @@ def tile_cgblock_pb_kernel(
                                 identity[:],
                             )
                     target = grouped_words[:, bank * 2 * P : (bank + 1) * 2 * P, :]
-                    if bank == 0:
+                    if bank == 0 and not (w_rows is s_w_rows and half == 1):
                         nc.vector.tensor_copy(out=target, in_=wt[:].rearrange("p u n -> p n u"))
                     else:
                         nc.scalar.copy(out=target, in_=wt[:].rearrange("p u n -> p n u"))
@@ -301,21 +358,26 @@ def tile_cgblock_pb_kernel(
         gate = consts.tile([P, OUTPUTS], F32, name="gate")
         gated_bias = consts.tile([P, OUTPUTS], F32, name="gated_bias")
         best = consts.tile([P, PAIR, OUTPUTS], F32, name="best")
-        gated_bias_ps = kept.tile([P, OUTPUTS - SPLIT], F32, name="gated_bias_ps")
+        bias_ps = {}
         gated = {}
 
         def open_gate():
             for half in range(HALVES):
-                cols = slice(half * N_TILE, (half + 1) * N_TILE)
+                cols = half_columns(half)
                 acc = project(CONTEXT, 0, c_w_codes, c_w_planes, half)
                 nc.vector.tensor_tensor(
-                    out=gate[:, cols], in0=acc[:], in1=c_bias_rows[:, cols], op=ALU.add
+                    out=gate[:, cols], in0=acc[:], in1=c_bias[:, cols], op=ALU.add
                 )
+            for half in range(HALVES):
+                cols = half_columns(half)
+                spread_ps = spread_bias(1, cols)
                 nc.vector.tensor_tensor(
-                    out=gated_bias[:, cols], in0=gate[:, cols], in1=s_bias_rows[:, cols], op=ALU.mult
+                    out=gated_bias[:, cols], in0=gate[:, cols], in1=spread_ps[:], op=ALU.mult
                 )
 
         def keep_gated_bias():
+            gated_bias_ps = kept.tile([P, OUTPUTS - SPLIT], F32, tag="kept", name="gated_bias_ps")
+            bias_ps[0] = gated_bias_ps
             nc.tensor.matmul(
                 gated_bias_ps[:], lhsT=identity[:], rhs=gated_bias[:, SPLIT:], start=True, stop=True
             )
@@ -325,7 +387,7 @@ def tile_cgblock_pb_kernel(
                 gated[pair] = best
             else:
                 gated[pair] = results.tile([P, PAIR, OUTPUTS], F32, tag="gated", name="gated")
-            for half in reversed(range(HALVES)):
+            for half in range(HALVES) if pair == PAIRS - 1 else reversed(range(HALVES)):
                 for s in range(PAIR):
                     cols = slice(half * N_TILE, (half + 1) * N_TILE)
                     acc = project(pair, s, s_w_codes, s_w_planes, half)
@@ -335,45 +397,87 @@ def tile_cgblock_pb_kernel(
 
         def add_bias_and_store(pair):
             slices = slice(pair * PAIR, (pair + 1) * PAIR)
-            first, source = (SPLIT, gated_bias_ps) if on_gpsimd(pair) else (0, gated_bias)
-            shape = [P, PAIR, OUTPUTS - first]
+            bias_cols = gated_bias[:, SPLIT:] if pair == 0 else bias_ps[0][:]
+            shape = [P, PAIR, OUTPUTS - SPLIT]
             biased = results.tile(shape, F32, tag="biased", name="biased")
             nc.vector.tensor_tensor(
                 out=biased[:],
-                in0=gated[pair][:, :, first:],
-                in1=source[:].unsqueeze(1).to_broadcast(shape),
+                in0=gated[pair][:, :, SPLIT:],
+                in1=bias_cols.unsqueeze(1).to_broadcast(shape),
                 op=ALU.add,
             )
-            nc.sync.dma_start(out=out_0[:, slices, first:], in_=biased[:])
+            nc.sync.dma_start(out=out_0[:, slices, SPLIT:], in_=biased[:])
 
-        def on_gpsimd(pair):
-            return 0 < pair < PAIRS - 1
-
-        def add_bias_in_place_and_store(pair):
+        def add_first_columns_and_store(pair):
             slices = slice(pair * PAIR, (pair + 1) * PAIR)
             part = gated[pair][:, :, :SPLIT]
+            if pair == 0:
+                first_sum = results.tile([P, PAIR, SPLIT], F32, tag="biased", name="first_sum")
+                target = first_sum[:]
+            else:
+                target = part
             nc.gpsimd.tensor_tensor(
-                out=part,
+                out=target,
                 in0=part,
                 in1=gated_bias[:, :SPLIT].unsqueeze(1).to_broadcast([P, PAIR, SPLIT]),
                 op=ALU.add,
             )
-            nc.sync.dma_start(out=out_0[:, slices, :SPLIT], in_=part)
+            nc.sync.dma_start(out=out_0[:, slices, :SPLIT], in_=target)
 
-        def pool(pair, s):
+        last_sums = {}
+
+        def open_last_sums():
+            for s in range(PAIR):
+                last_sums[s] = turned.tile([P, SPLIT], F32, tag="turned", name="last_sum")
+                nc.tensor.matmul(
+                    last_sums[s][:], lhsT=identity[:], rhs=gated_bias[:, :SPLIT], start=True, stop=False
+                )
+
+        def close_last_sums_and_store(pair):
+            for s in range(PAIR):
+                nc.tensor.matmul(
+                    last_sums[s][:], lhsT=identity[:], rhs=gated[pair][:, s, :SPLIT], start=False, stop=True
+                )
+                last_sum = results.tile([P, SPLIT], F32, tag="last_sum_rows", name="last_sum_rows")
+                nc.scalar.copy(out=last_sum[:], in_=last_sums[s][:])
+                nc.sync.dma_start(out=out_0[:, pair * PAIR + s, :SPLIT], in_=last_sum[:])
+
+        def pool(pair, cols):
             if pair > 0:
                 nc.vector.tensor_tensor(
-                    out=best[:, s, :], in0=best[:, s, :], in1=gated[pair][:, s, :], op=ALU.max
+                    out=best[:, :, cols],
+                    in0=best[:, :, cols],
+                    in1=gated[pair][:, :, cols],
+                    op=ALU.max,
                 )
+
+        pooled = consts.tile([P, OUTPUTS], F32, name="pooled")
+
+        def join_slices(cols):
+            nc.vector.tensor_tensor(
+                out=pooled[:, cols], in0=best[:, 0, cols], in1=best[:, 1, cols], op=ALU.max
+            )
+
+        def add_bias_to_best_and_store(cols):
+            nc.vector.tensor_tensor(
+                out=pooled[:, cols], in0=pooled[:, cols], in1=gated_bias[:, cols], op=ALU.add
+            )
+            nc.sync.dma_start(out=out_1[:, cols], in_=pooled[:, cols])
 
         def step(n):
             if n == CONTEXT:
                 open_gate()
+            if n == PAIRS - 1:
+                open_last_sums()
             if n >= 0:
                 multiply(n)
             if n == 0:
                 keep_gated_bias()
-            if size_of(n + 2):
+            if n == PAIRS - 1:
+                close_last_sums_and_store(n)
+            if size_of(n + 2) and by_vector(n + 2):
+                measure(n + 2)
+            elif size_of(n + 2):
                 take_means(n + 2)
                 spread(n + 2)
             for s in range(PAIR):
@@ -383,29 +487,33 @@ def tile_cgblock_pb_kernel(
                     turn(n + 3, s)
             if size_of(n + 1):
                 regroup_last_columns(n + 1)
+            if n == PAIRS - 1:
+                return
             long_steps = []
             if n >= 0:
                 long_steps.append(lambda: add_bias_and_store(n))
-            if size_of(n + 1):
+            if size_of(n + 1) and scalar_columns(n + 1):
                 long_steps.append(lambda: regroup_first_columns(n + 1))
+            if n >= 0:
+                long_steps.append(lambda: pool(n, slice(POOLED_FIRST, OUTPUTS)))
             if size_of(n + 1):
                 long_steps.append(lambda: quantise(n + 1))
             if n >= 0:
-                long_steps.append(lambda: pool(n, 0))
-                long_steps.append(lambda: pool(n, 1))
+                long_steps.append(lambda: pool(n, slice(0, POOLED_FIRST)))
             short_steps = coefficient_steps(n + 2) if size_of(n + 2) else []
             for k in range(max(len(long_steps), len(short_steps))):
                 if k < len(long_steps):
                     long_steps[k]()
                 if k < len(short_steps):
                     short_steps[k]()
-            if on_gpsimd(n):
-                add_bias_in_place_and_store(n)
+            if n >= 0:
+                add_first_columns_and_store(n)
 
         step(CONTEXT - 3)
         step(CONTEXT - 2)
         for half in range(HALVES):
             quantise_weight_half(c_w_rows, c_w_codes, c_w_planes, half)
+        spread_context_bias()
         step(CONTEXT - 1)
         for half in range(HALVES):
             quantise_weight_half(s_w_rows, s_w_codes, s_w_planes, half)
@@ -413,8 +521,12 @@ def tile_cgblock_pb_kernel(
         with tc.manual_schedule():
             for n in range(PAIRS):
                 step(n)
-
-        pooled = results.tile([P, OUTPUTS], F32, tag="biased", name="pooled")
-        nc.vector.tensor_tensor(out=pooled[:], in0=best[:, 0, :], in1=best[:, 1, :], op=ALU.max)
-        nc.vector.tensor_tensor(out=pooled[:], in0=pooled[:], in1=gated_bias[:], op=ALU.add)
-        nc.sync.dma_start(out=out_1, in_=pooled[:])
+            last = PAIRS - 1
+            first_half, last_half = (slice(h * N_TILE, (h + 1) * N_TILE) for h in range(HALVES))
+            pool(last, first_half)
+            add_bias_and_store(last)
+            join_slices(first_half)
+            pool(last, last_half)
+            add_bias_to_best_and_store(first_half)
+            join_slices(last_half)
+            add_bias_to_best_and_store(last_half)

@@ -26,7 +26,6 @@ PAIR = 2
 PAIRS = SLICES // PAIR
 CONTEXT = -1
 CHUNK = 4
-POOLED_FIRST = 3 * OUTPUTS // 4
 BN_WORDS = 6
 SPLIT = N_TILE
 
@@ -147,17 +146,14 @@ def tile_cgblock_pb_kernel(
         def by_vector(group):
             return group in (CONTEXT, 0)
 
-        xts, mean_ps, neg_mean, moments, std = {}, {}, {}, {}, {}
+        xts, mean_ps, neg_mean, sq_sum, moments, std = {}, {}, {}, {}, {}, {}
         scale, bias, hidden, grouped, codes, planes = {}, {}, {}, {}, {}, {}
 
         def turn(group, s):
             rows = blocks_of(group)[s]
             if s == 0:
                 xts[group] = []
-                if not by_vector(group):
-                    mean_ps[group] = products.tile(
-                        [P, size_of(group), PER_PARTITION], F32, tag="acc", name="mean_ps"
-                    )
+                mean_ps[group] = []
             words = rows.bitcast(F32)
             xt = turned.tile([P, QUARTERS, P], F32, tag="turned", name="xt")
             for q in range(QUARTERS):
@@ -165,20 +161,24 @@ def tile_cgblock_pb_kernel(
             xts[group].append(xt)
             if by_vector(group):
                 return
+            means = products.tile([P, PER_PARTITION], F32, tag="acc", name="means")
+            mean_ps[group].append(means)
             by_place = rows.rearrange("b (g p t) -> b g t p", g=PASSES, t=PACK)
             for j in range(PER_PARTITION):
                 nc.tensor.matmul(
-                    mean_ps[group][:, s, j : j + 1],
+                    means[:, j : j + 1],
                     lhsT=by_place[:, j // PACK, j % PACK, :],
                     rhs=minus_inv_batch[:],
                     start=True,
                     stop=True,
                 )
 
-        def take_means(group):
-            shape = [P, size_of(group), PER_PARTITION]
-            neg_mean[group] = stats.tile(shape, F32, tag="neg_mean", name="neg_mean")
-            nc.scalar.copy(out=neg_mean[group][:], in_=mean_ps[group][:])
+        def take_means(group, s):
+            if s == 0:
+                shape = [P, size_of(group), PER_PARTITION]
+                neg_mean[group] = stats.tile(shape, F32, tag="neg_mean", name="neg_mean")
+                sq_sum[group] = stats.tile(shape, F32, tag="sq_sum", name="sq_sum")
+            nc.scalar.copy(out=neg_mean[group][:, s, :], in_=mean_ps[group][s][:])
 
         def measure(group):
             shape = [P, size_of(group), QUARTERS, BN_WORDS]
@@ -202,25 +202,26 @@ def tile_cgblock_pb_kernel(
         def by_q(tile):
             return tile[:].rearrange("p s (q e) -> p s q e", e=2)
 
-        def spread(group):
-            shape = [P, size_of(group), PER_PARTITION]
-            sq_sum = stats.tile(shape, F32, tag="sq_sum", name="sq_sum")
-            for s, xt in enumerate(xts[group]):
-                squares = stage.tile([P, PER_PARTITION, P], BF16, tag="squares", name="squares")
-                for q in range(QUARTERS):
-                    for e in range(2):
-                        j = 2 * q + e
-                        nc.scalar.activation(
-                            out=squares[:, j, :],
-                            in_=halves_of(xt)[:, q, e, :],
-                            func=ACT.Square,
-                            bias=neg_mean[group][:, s, j : j + 1],
-                            scale=1.0,
-                            accum_out=sq_sum[:, s, j : j + 1],
-                        )
-            std[group] = stats.tile(shape, F32, tag="std", name="std")
+        def spread(group, s):
+            squares = stage.tile([P, PER_PARTITION, P], BF16, tag="squares", name="squares")
+            for q in range(QUARTERS):
+                for e in range(2):
+                    j = 2 * q + e
+                    nc.scalar.activation(
+                        out=squares[:, j, :],
+                        in_=halves_of(xts[group][s])[:, q, e, :],
+                        func=ACT.Square,
+                        bias=neg_mean[group][:, s, j : j + 1],
+                        scale=1.0,
+                        accum_out=sq_sum[group][:, s, j : j + 1],
+                    )
+
+        def take_root(group):
+            std[group] = stats.tile(
+                [P, size_of(group), PER_PARTITION], F32, tag="std", name="std"
+            )
             nc.scalar.activation(
-                out=std[group][:], in_=sq_sum[:], func=ACT.Sqrt, bias=eps[:], scale=1.0 / P
+                out=std[group][:], in_=sq_sum[group][:], func=ACT.Sqrt, bias=eps[:], scale=1.0 / P
             )
 
         def coefficient_steps(group):
@@ -360,6 +361,7 @@ def tile_cgblock_pb_kernel(
         best = consts.tile([P, PAIR, OUTPUTS], F32, name="best")
         bias_ps = {}
         gated = {}
+        products_left = []
 
         def open_gate():
             for half in range(HALVES):
@@ -389,11 +391,16 @@ def tile_cgblock_pb_kernel(
                 gated[pair] = results.tile([P, PAIR, OUTPUTS], F32, tag="gated", name="gated")
             for half in range(HALVES) if pair == PAIRS - 1 else reversed(range(HALVES)):
                 for s in range(PAIR):
-                    cols = slice(half * N_TILE, (half + 1) * N_TILE)
                     acc = project(pair, s, s_w_codes, s_w_planes, half)
-                    nc.vector.tensor_tensor(
-                        out=gated[pair][:, s, cols], in0=acc[:], in1=gate[:, cols], op=ALU.mult
-                    )
+                    products_left.append((acc, s, half_columns(half)))
+            for i in range(2 * PAIR if pair == PAIRS - 1 else 2 * PAIR - 1):
+                gate_next(pair)
+
+        def gate_next(pair):
+            acc, s, cols = products_left.pop(0)
+            nc.vector.tensor_tensor(
+                out=gated[pair][:, s, cols], in0=acc[:], in1=gate[:, cols], op=ALU.mult
+            )
 
         def add_bias_and_store(pair):
             slices = slice(pair * PAIR, (pair + 1) * PAIR)
@@ -442,12 +449,12 @@ def tile_cgblock_pb_kernel(
                 nc.scalar.copy(out=last_sum[:], in_=last_sums[s][:])
                 nc.sync.dma_start(out=out_0[:, pair * PAIR + s, :SPLIT], in_=last_sum[:])
 
-        def pool(pair, cols):
+        def pool(pair, s, cols):
             if pair > 0:
                 nc.vector.tensor_tensor(
-                    out=best[:, :, cols],
-                    in0=best[:, :, cols],
-                    in1=gated[pair][:, :, cols],
+                    out=best[:, s, cols],
+                    in0=best[:, s, cols],
+                    in1=gated[pair][:, s, cols],
                     op=ALU.max,
                 )
 
@@ -478,8 +485,8 @@ def tile_cgblock_pb_kernel(
             if size_of(n + 2) and by_vector(n + 2):
                 measure(n + 2)
             elif size_of(n + 2):
-                take_means(n + 2)
-                spread(n + 2)
+                spread(n + 2, 1)
+                take_root(n + 2)
             for s in range(PAIR):
                 if s < size_of(n + 1):
                     activate(n + 1, s)
@@ -487,6 +494,10 @@ def tile_cgblock_pb_kernel(
                     turn(n + 3, s)
             if size_of(n + 1):
                 regroup_last_columns(n + 1)
+            if size_of(n + 3) and not by_vector(n + 3):
+                take_means(n + 3, 0)
+                spread(n + 3, 0)
+                take_means(n + 3, 1)
             if n == PAIRS - 1:
                 return
             long_steps = []
@@ -495,11 +506,12 @@ def tile_cgblock_pb_kernel(
             if size_of(n + 1) and scalar_columns(n + 1):
                 long_steps.append(lambda: regroup_first_columns(n + 1))
             if n >= 0:
-                long_steps.append(lambda: pool(n, slice(POOLED_FIRST, OUTPUTS)))
+                long_steps.append(lambda: gate_next(n))
             if size_of(n + 1):
                 long_steps.append(lambda: quantise(n + 1))
             if n >= 0:
-                long_steps.append(lambda: pool(n, slice(0, POOLED_FIRST)))
+                long_steps.append(lambda: pool(n, 0, slice(0, OUTPUTS)))
+                long_steps.append(lambda: pool(n, 1, slice(0, OUTPUTS)))
             short_steps = coefficient_steps(n + 2) if size_of(n + 2) else []
             for k in range(max(len(long_steps), len(short_steps))):
                 if k < len(long_steps):
@@ -523,10 +535,12 @@ def tile_cgblock_pb_kernel(
                 step(n)
             last = PAIRS - 1
             first_half, last_half = (slice(h * N_TILE, (h + 1) * N_TILE) for h in range(HALVES))
-            pool(last, first_half)
+            for s in range(PAIR):
+                pool(last, s, first_half)
             add_bias_and_store(last)
             join_slices(first_half)
-            pool(last, last_half)
+            for s in range(PAIR):
+                pool(last, s, last_half)
             add_bias_to_best_and_store(first_half)
             join_slices(last_half)
             add_bias_to_best_and_store(last_half)

@@ -393,7 +393,7 @@ def tile_cgblock_pb_kernel(
                 for s in range(PAIR):
                     acc = project(pair, s, s_w_codes, s_w_planes, half)
                     products_left.append((acc, s, half_columns(half)))
-            for i in range(2 * PAIR if pair == PAIRS - 1 else 2 * PAIR - 1):
+            for i in range(2 * PAIR if pair == PAIRS - 1 else PAIR):
                 gate_next(pair)
 
         def gate_next(pair):
@@ -402,34 +402,28 @@ def tile_cgblock_pb_kernel(
                 out=gated[pair][:, s, cols], in0=acc[:], in1=gate[:, cols], op=ALU.mult
             )
 
-        def add_bias_and_store(pair):
-            slices = slice(pair * PAIR, (pair + 1) * PAIR)
-            bias_cols = gated_bias[:, SPLIT:] if pair == 0 else bias_ps[0][:]
-            shape = [P, PAIR, OUTPUTS - SPLIT]
-            biased = results.tile(shape, F32, tag="biased", name="biased")
-            nc.vector.tensor_tensor(
-                out=biased[:],
-                in0=gated[pair][:, :, SPLIT:],
-                in1=bias_cols.unsqueeze(1).to_broadcast(shape),
-                op=ALU.add,
-            )
-            nc.sync.dma_start(out=out_0[:, slices, SPLIT:], in_=biased[:])
+        def add_bias_steps(pair):
+            first, bias_cols = (0, gated_bias[:]) if pair == 0 else (SPLIT, bias_ps[0][:])
+
+            def add(s):
+                biased = results.tile([P, OUTPUTS - first], F32, tag="biased", name="biased")
+                nc.vector.tensor_tensor(
+                    out=biased[:], in0=gated[pair][:, s, first:], in1=bias_cols, op=ALU.add
+                )
+                nc.sync.dma_start(out=out_0[:, pair * PAIR + s, first:], in_=biased[:])
+
+            return [lambda s=s: add(s) for s in range(PAIR)]
 
         def add_first_columns_and_store(pair):
             slices = slice(pair * PAIR, (pair + 1) * PAIR)
             part = gated[pair][:, :, :SPLIT]
-            if pair == 0:
-                first_sum = results.tile([P, PAIR, SPLIT], F32, tag="biased", name="first_sum")
-                target = first_sum[:]
-            else:
-                target = part
             nc.gpsimd.tensor_tensor(
-                out=target,
+                out=part,
                 in0=part,
                 in1=gated_bias[:, :SPLIT].unsqueeze(1).to_broadcast([P, PAIR, SPLIT]),
                 op=ALU.add,
             )
-            nc.sync.dma_start(out=out_0[:, slices, :SPLIT], in_=target)
+            nc.sync.dma_start(out=out_0[:, slices, :SPLIT], in_=part)
 
         last_sums = {}
 
@@ -502,23 +496,30 @@ def tile_cgblock_pb_kernel(
                 return
             long_steps = []
             if n >= 0:
-                long_steps.append(lambda: add_bias_and_store(n))
+                bias_steps = add_bias_steps(n)
+                gate_step = lambda: gate_next(n)
+            if n == 0:
+                long_steps += [gate_step, gate_step, bias_steps[0]]
+            elif n > 0:
+                long_steps += [bias_steps[0], gate_step, bias_steps[1]]
+            before_regrouping = max(len(long_steps) - 1, 0)
             if size_of(n + 1) and scalar_columns(n + 1):
                 long_steps.append(lambda: regroup_first_columns(n + 1))
-            if n >= 0:
-                long_steps.append(lambda: gate_next(n))
+            if n > 0:
+                long_steps.append(gate_step)
             if size_of(n + 1):
                 long_steps.append(lambda: quantise(n + 1))
-            if n >= 0:
-                long_steps.append(lambda: pool(n, 0, slice(0, OUTPUTS)))
-                long_steps.append(lambda: pool(n, 1, slice(0, OUTPUTS)))
+            if n == 0:
+                long_steps.append(bias_steps[1])
+            elif n > 0:
+                long_steps += [lambda s=s: pool(n, s, slice(0, OUTPUTS)) for s in range(PAIR)]
             short_steps = coefficient_steps(n + 2) if size_of(n + 2) else []
-            for k in range(max(len(long_steps), len(short_steps))):
+            for k in range(max(len(long_steps), before_regrouping + len(short_steps))):
                 if k < len(long_steps):
                     long_steps[k]()
-                if k < len(short_steps):
-                    short_steps[k]()
-            if n >= 0:
+                if 0 <= k - before_regrouping < len(short_steps):
+                    short_steps[k - before_regrouping]()
+            if n > 0:
                 add_first_columns_and_store(n)
 
         step(CONTEXT - 3)
@@ -537,7 +538,8 @@ def tile_cgblock_pb_kernel(
             first_half, last_half = (slice(h * N_TILE, (h + 1) * N_TILE) for h in range(HALVES))
             for s in range(PAIR):
                 pool(last, s, first_half)
-            add_bias_and_store(last)
+            for add_bias in add_bias_steps(last):
+                add_bias()
             join_slices(first_half)
             for s in range(PAIR):
                 pool(last, s, last_half)

from contextlib import ExitStack

import concourse.mybir as mybir
from concourse.masks import make_identity

F32 = mybir.dt.float32
BF16 = mybir.dt.bfloat16
U32 = mybir.dt.uint32
U8 = mybir.dt.uint8
FP8X4 = mybir.dt.float8_e4m3fn_x4
ACT = mybir.ActivationFunctionType
ALU = mybir.AluOpType

P = 128
SLICES = 32
FEATURES = 1024
OUTPUTS = 1024
EPS = 1e-5
PACK = 4
PASSES = FEATURES // (P * PACK)
QUARTERS = FEATURES // (2 * P)
PER_PARTITION = FEATURES // P
N_TILE = 512
HALVES = OUTPUTS // N_TILE
PAIR = 2
PAIRS = SLICES // PAIR
CONTEXT = -1
CHUNK = 4
BN_WORDS = 6
SPLIT = N_TILE

FLOPS = 2 * (SLICES + 1) * P * FEATURES * OUTPUTS


def tile_cgblock_pb_kernel(
    tc, s_z2, c_z2, s_g2, s_be2, s_w3, s_b3, c_g2, c_be2, c_w3, c_b3, out_0, out_1
):
    nc = tc.nc
    with ExitStack() as ctx:
        consts = ctx.enter_context(tc.tile_pool(name="consts", bufs=1))
        inputs = ctx.enter_context(tc.tile_pool(name="inputs", bufs=1))
        weights = ctx.enter_context(tc.tile_pool(name="weights", bufs=1))
        stage = ctx.enter_context(tc.tile_pool(name="stage", bufs=2))
        stats = ctx.enter_context(tc.tile_pool(name="stats", bufs=3))
        quantised = ctx.enter_context(tc.tile_pool(name="quantised", bufs=4))
        results = ctx.enter_context(tc.tile_pool(name="results", bufs=3))
        turned = ctx.enter_context(tc.psum_pool(name="turned", bufs=4))
        kept = ctx.enter_context(tc.psum_pool(name="kept", bufs=1))
        products = ctx.enter_context(tc.psum_pool(name="products", bufs=3))

        identity = consts.tile([P, P], F32, name="identity")
        make_identity(nc, identity[:])
        minus_inv_batch = consts.tile([P, 1], BF16, name="minus_inv_batch")
        nc.vector.memset(minus_inv_batch[:], -1.0 / P)
        eps = consts.tile([P, 1], F32, name="eps")
        nc.vector.memset(eps[:], EPS)
        warm = consts.tile([P, 1], F32, name="warm")
        nc.scalar.activation(out=warm[:], in_=eps[:], func=ACT.Sqrt)

        vector_rows = consts.tile([P, 2 * P], F32, name="vector_rows")
        nc.vector.memset(vector_rows[:], 0.0)
        for v, vector in enumerate((s_g2, s_be2, c_g2, c_be2)):
            nc.sync.dma_start(
                out=vector_rows[:].bitcast(BF16)[PASSES * v : PASSES * (v + 1), :],
                in_=vector.rearrange("(g w) -> g w", g=PASSES),
            )

        s_blocks = []

        def load_slices(size):
            first = len(s_blocks)
            rows = inputs.tile([P, size, FEATURES], BF16, name="s_rows%d" % first)
            nc.sync.dma_start(out=rows[:], in_=s_z2[:, first : first + size, :])
            for s in range(size):
                s_blocks.append(rows[:, s, :])

        def load_weight(w, label):
            halves = []
            for half in range(HALVES):
                rows = inputs.tile([P, N_TILE // P, FEATURES], BF16, name="%s%d" % (label, half))
                nc.sync.dma_start(
                    out=rows[:],
                    in_=w[half * N_TILE : (half + 1) * N_TILE, :].rearrange("(c p) k -> p c k", p=P),
                )
                halves.append(rows)
            return halves

        bias_rows = consts.tile([P, 2, OUTPUTS], BF16, name="bias_rows")
        nc.gpsimd.memset(bias_rows[:], 0.0)
        c_rows = inputs.tile([P, FEATURES], BF16, name="c_rows")
        nc.sync.dma_start(out=c_rows[:], in_=c_z2)
        load_slices(PAIR)
        c_w_rows = load_weight(c_w3, "c_w_rows")
        for v, vector in enumerate((c_b3, s_b3)):
            nc.sync.dma_start(out=bias_rows[0:1, v, :], in_=vector.unsqueeze(0))
        load_slices(PAIR)
        s_w_rows = load_weight(s_w3, "s_w_rows")
        while len(s_blocks) < SLICES:
            load_slices(CHUNK)
        ones = consts.tile([P, P], BF16, name="ones")
        nc.gpsimd.memset(ones[:], 1.0)
        c_bias = consts.tile([P, OUTPUTS], F32, name="c_bias")

        def spread_bias(v, cols):
            spread_ps = kept.tile([P, N_TILE], F32, tag="kept", name="spread_ps")
            nc.tensor.matmul(
                spread_ps[:], lhsT=ones[:], rhs=bias_rows[:, v, cols], start=True, stop=True
            )
            return spread_ps

        def half_columns(half):
            return slice(half * N_TILE, (half + 1) * N_TILE)

        def spread_context_bias():
            for half in range(HALVES):
                spread_ps = spread_bias(0, half_columns(half))
                nc.scalar.copy(out=c_bias[:, half_columns(half)], in_=spread_ps[:])

        tables_ps = turned.tile([P, QUARTERS, P], F32, tag="turned", name="tables_ps")
        tables = consts.tile([P, 4, PER_PARTITION], F32, name="tables")
        spread_tables = tables[:].rearrange("p v (g u e) -> p u (v g) e", g=PASSES, u=2)
        for u in range(2):
            nc.tensor.transpose(tables_ps[:, u, :], vector_rows[:, u : 2 * P : 2], identity[:])
            nc.vector.tensor_copy(
                out=spread_tables[:, u, :, :],
                in_=tables_ps[:, u, 0 : 4 * PASSES].bitcast(BF16).rearrange("p (r e) -> p r e", e=2),
            )
        s_gain, s_shift = tables[:, 0, :], tables[:, 1, :]
        c_gain, c_shift = tables[:, 2, :], tables[:, 3, :]

        def every_second(words, q):
            first = (q // 2) * 2 * P + q % 2
            return words[:, first : (q // 2 + 1) * 2 * P : 2]

        def halves_of(xt):
            return xt[:].bitcast(BF16).rearrange("p q (b e) -> p q e b", e=2)

        def blocks_of(group):
            if group == CONTEXT:
                return [c_rows[:]]
            return s_blocks[group * PAIR : (group + 1) * PAIR]

        def size_of(group):
            return len(blocks_of(group)) if CONTEXT <= group < PAIRS else 0

        def by_vector(group):
            return group in (CONTEXT, 0)

        xts, mean_ps, neg_mean, sq_sum, moments, std = {}, {}, {}, {}, {}, {}
        scale, bias, hidden, grouped, codes, planes = {}, {}, {}, {}, {}, {}

        def turn(group, s):
            rows = blocks_of(group)[s]
            if s == 0:
                xts[group] = []
                mean_ps[group] = []
            words = rows.bitcast(F32)
            xt = turned.tile([P, QUARTERS, P], F32, tag="turned", name="xt")
            for q in range(QUARTERS):
                nc.tensor.transpose(xt[:, q, :], every_second(words, q), identity[:])
            xts[group].append(xt)
            if by_vector(group):
                return
            means = products.tile([P, PER_PARTITION], F32, tag="acc", name="means")
            mean_ps[group].append(means)
            by_place = rows.rearrange("b (g p t) -> b g t p", g=PASSES, t=PACK)
            for j in range(PER_PARTITION):
                nc.tensor.matmul(
                    means[:, j : j + 1],
                    lhsT=by_place[:, j // PACK, j % PACK, :],
                    rhs=minus_inv_batch[:],
                    start=True,
                    stop=True,
                )

        def take_means(group, s):
            if s == 0:
                shape = [P, size_of(group), PER_PARTITION]
                neg_mean[group] = stats.tile(shape, F32, tag="neg_mean", name="neg_mean")
                sq_sum[group] = stats.tile(shape, F32, tag="sq_sum", name="sq_sum")
            nc.scalar.copy(out=neg_mean[group][:, s, :], in_=mean_ps[group][s][:])

        def measure(group):
            shape = [P, size_of(group), QUARTERS, BN_WORDS]
            moments[group] = stats.tile(shape, F32, tag="moments", name="moments")
            for s, xt in enumerate(xts[group]):
                for q in range(QUARTERS):
                    nc.vector.bn_stats(
                        out=moments[group][:, s, q, :], in_=xt[:, q, :].bitcast(BF16)
                    )
            std[group] = stats.tile(
                [P, size_of(group), PER_PARTITION], F32, tag="std", name="std"
            )
            nc.scalar.activation(
                out=by_q(std[group]),
                in_=moments[group][:, :, :, 2:BN_WORDS:3],
                func=ACT.Sqrt,
                bias=eps[:],
                scale=1.0 / P,
            )

        def by_q(tile):
            return tile[:].rearrange("p s (q e) -> p s q e", e=2)

        def spread(group, s):
            squares = stage.tile([P, PER_PARTITION, P], BF16, tag="squares", name="squares")
            for q in range(QUARTERS):
                for e in range(2):
                    j = 2 * q + e
                    nc.scalar.activation(
                        out=squares[:, j, :],
                        in_=halves_of(xts[group][s])[:, q, e, :],
                        func=ACT.Square,
                        bias=neg_mean[group][:, s, j : j + 1],
                        scale=1.0,
                        accum_out=sq_sum[group][:, s, j : j + 1],
                    )

        def take_root(group):
            std[group] = stats.tile(
                [P, size_of(group), PER_PARTITION], F32, tag="std", name="std"
            )
            nc.scalar.activation(
                out=std[group][:], in_=sq_sum[group][:], func=ACT.Sqrt, bias=eps[:], scale=1.0 / P
            )

        def coefficient_steps(group):
            shape = [P, size_of(group), PER_PARTITION]
            gain, shift = (c_gain, c_shift) if group == CONTEXT else (s_gain, s_shift)
            inv_std = stats.tile(shape, F32, tag="inv_std", name="inv_std")
            centre = stats.tile(shape, F32, tag="centre", name="centre")
            scale[group] = stats.tile(shape, F32, tag="scale", name="scale")
            bias[group] = stats.tile(shape, F32, tag="bias", name="bias")
            if by_vector(group):
                means, sign = moments[group][:, :, :, 1:BN_WORDS:3], ALU.subtract
            else:
                means, sign = by_q(neg_mean[group]), ALU.add
            return [
                lambda: nc.vector.reciprocal(out=inv_std[:], in_=std[group][:]),
                lambda: nc.vector.tensor_tensor(
                    out=scale[group][:],
                    in0=inv_std[:],
                    in1=gain.unsqueeze(1).to_broadcast(shape),
                    op=ALU.mult,
                ),
                lambda: nc.vector.tensor_tensor(
                    out=by_q(centre), in0=means, in1=by_q(scale[group]), op=ALU.mult
                ),
                lambda: nc.vector.tensor_tensor(
                    out=bias[group][:],
                    in0=shift.unsqueeze(1).to_broadcast(shape),
                    in1=centre[:],
                    op=sign,
                ),
            ]

        def activate(group, s):
            if s == 0:
                width = size_of(group) * PASSES * P
                hidden[group] = stage.tile([P, PACK, width], BF16, tag="hidden", name="hidden")
            for q in range(QUARTERS):
                for e in range(2):
                    j = 2 * q + e
                    g, t = j // PACK, j % PACK
                    first = (s * PASSES + g) * P
                    nc.scalar.activation(
                        out=hidden[group][:, t, first : first + P],
                        in_=halves_of(xts[group][s])[:, q, e, :],
                        func=ACT.Relu,
                        bias=bias[group][:, s, j : j + 1],
                        scale=scale[group][:, s, j : j + 1],
                    )

        def scalar_columns(group):
            width = size_of(group) * PASSES * P
            return 0 if group == PAIRS - 1 else 3 * width // 4

        def regroup_last_columns(group):
            width = size_of(group) * PASSES * P
            middle = scalar_columns(group)
            grouped[group] = stage.tile(
                [P, width, PACK], BF16, tag="grouped", name="grouped", align_bytes=64
            )
            nc.scalar.copy(
                out=grouped[group][:, middle:, :].rearrange("p (c i) t -> p c t i", i=4),
                in_=hidden[group][:, :, middle:].rearrange("p t (c i) -> p c t i", i=4),
            )

        def regroup_first_columns(group):
            middle = scalar_columns(group)
            nc.vector.tensor_copy(
                out=grouped[group][:, :middle, :].rearrange("p (c i) t -> p c t i", i=4),
                in_=hidden[group][:, :, :middle].rearrange("p t (c i) -> p c t i", i=4),
            )

        def quantise(group):
            width = size_of(group) * PASSES * P
            codes[group] = quantised.tile([P, width], U32, tag="codes", name="codes", align_bytes=64)
            planes[group] = quantised.tile([P, width], U8, tag="planes", name="planes", align_bytes=64)
            nc.vector.quantize_mx(
                out=codes[group][:].bitcast(FP8X4),
                scales=planes[group][:],
                in_=grouped[group][:].rearrange("p w t -> p (w t)"),
            )

        def weight_tiles(label):
            w_codes = weights.tile([P, PASSES, OUTPUTS], U32, name=label + "_codes", align_bytes=64)
            w_planes = weights.tile([P, PASSES, OUTPUTS], U8, name=label + "_planes", align_bytes=64)
            return w_codes, w_planes

        def quantise_weight_half(w_rows, w_codes, w_planes, half):
            words = w_rows[half][:].bitcast(F32)
            cols = slice(half * N_TILE, (half + 1) * N_TILE)
            for g in range(PASSES):
                grouped = stage.tile(
                    [P, N_TILE, PACK], BF16, tag="w_grouped", name="w_grouped", align_bytes=64
                )
                grouped_words = grouped[:].bitcast(F32)
                for bank in range(2):
                    wt = products.tile([P, 2, 2 * P], F32, tag="acc", name="wt")
                    for u in range(2):
                        q = 2 * g + u
                        for c in range(2):
                            nc.tensor.transpose(
                                wt[:, u, c * P : (c + 1) * P],
                                every_second(words[:, 2 * bank + c, :], q),
                                identity[:],
                            )
                    target = grouped_words[:, bank * 2 * P : (bank + 1) * 2 * P, :]
                    if bank == 0 and not (w_rows is s_w_rows and half == 1):
                        nc.vector.tensor_copy(out=target, in_=wt[:].rearrange("p u n -> p n u"))
                    else:
                        nc.scalar.copy(out=target, in_=wt[:].rearrange("p u n -> p n u"))
                nc.vector.quantize_mx(
                    out=w_codes[:, g, cols].bitcast(FP8X4),
                    scales=w_planes[:, g, cols],
                    in_=grouped[:].rearrange("p n t -> p (n t)"),
                )

        def project(group, s, w_codes, w_planes, half):
            acc = products.tile([P, N_TILE], F32, tag="acc", name="acc")
            cols = slice(half * N_TILE, (half + 1) * N_TILE)
            for g in range(PASSES):
                rows = slice((s * PASSES + g) * P, (s * PASSES + g + 1) * P)
                nc.tensor.matmul_mx(
                    out=acc[:],
                    lhsT=codes[group][:, rows].bitcast(FP8X4),
                    lhsT_scale=planes[group][:, rows],
                    rhs=w_codes[:, g, cols].bitcast(FP8X4),
                    rhs_scale=w_planes[:, g, cols],
                    start=(g == 0),
                    stop=(g == PASSES - 1),
                )
            return acc

        c_w_codes, c_w_planes = weight_tiles("c_w")
        s_w_codes, s_w_planes = weight_tiles("s_w")

        gate = consts.tile([P, OUTPUTS], F32, name="gate")
        gated_bias = consts.tile([P, OUTPUTS], F32, name="gated_bias")
        best = consts.tile([P, PAIR, OUTPUTS], F32, name="best")
        bias_ps = {}
        gated = {}
        products_left = []

        def open_gate():
            for half in range(HALVES):
                cols = half_columns(half)
                acc = project(CONTEXT, 0, c_w_codes, c_w_planes, half)
                nc.vector.tensor_tensor(
                    out=gate[:, cols], in0=acc[:], in1=c_bias[:, cols], op=ALU.add
                )
            for half in range(HALVES):
                cols = half_columns(half)
                spread_ps = spread_bias(1, cols)
                nc.vector.tensor_tensor(
                    out=gated_bias[:, cols], in0=gate[:, cols], in1=spread_ps[:], op=ALU.mult
                )

        def keep_gated_bias():
            gated_bias_ps = kept.tile([P, OUTPUTS - SPLIT], F32, tag="kept", name="gated_bias_ps")
            bias_ps[0] = gated_bias_ps
            nc.tensor.matmul(
                gated_bias_ps[:], lhsT=identity[:], rhs=gated_bias[:, SPLIT:], start=True, stop=True
            )

        def multiply(pair):
            if pair == 0:
                gated[pair] = best
            else:
                gated[pair] = results.tile([P, PAIR, OUTPUTS], F32, tag="gated", name="gated")
            for half in range(HALVES) if pair == PAIRS - 1 else reversed(range(HALVES)):
                for s in range(PAIR):
                    acc = project(pair, s, s_w_codes, s_w_planes, half)
                    products_left.append((acc, s, half_columns(half)))
            for i in range(2 * PAIR if pair == PAIRS - 1 else PAIR):
                gate_next(pair)

        def gate_next(pair):
            acc, s, cols = products_left.pop(0)
            nc.vector.tensor_tensor(
                out=gated[pair][:, s, cols], in0=acc[:], in1=gate[:, cols], op=ALU.mult
            )

        def add_bias_steps(pair):
            first, bias_cols = (0, gated_bias[:]) if pair == 0 else (SPLIT, bias_ps[0][:])

            def add(s):
                biased = results.tile([P, OUTPUTS - first], F32, tag="biased", name="biased")
                nc.vector.tensor_tensor(
                    out=biased[:], in0=gated[pair][:, s, first:], in1=bias_cols, op=ALU.add
                )
                nc.sync.dma_start(out=out_0[:, pair * PAIR + s, first:], in_=biased[:])

            return [lambda s=s: add(s) for s in range(PAIR)]

        def add_first_columns_and_store(pair):
            slices = slice(pair * PAIR, (pair + 1) * PAIR)
            part = gated[pair][:, :, :SPLIT]
            nc.gpsimd.tensor_tensor(
                out=part,
                in0=part,
                in1=gated_bias[:, :SPLIT].unsqueeze(1).to_broadcast([P, PAIR, SPLIT]),
                op=ALU.add,
            )
            nc.sync.dma_start(out=out_0[:, slices, :SPLIT], in_=part)

        last_sums = {}

        def open_last_sums():
            for s in range(PAIR):
                last_sums[s] = turned.tile([P, SPLIT], F32, tag="turned", name="last_sum")
                nc.tensor.matmul(
                    last_sums[s][:], lhsT=identity[:], rhs=gated_bias[:, :SPLIT], start=True, stop=False
                )

        def close_last_sums_and_store(pair):
            for s in range(PAIR):
                nc.tensor.matmul(
                    last_sums[s][:], lhsT=identity[:], rhs=gated[pair][:, s, :SPLIT], start=False, stop=True
                )
                last_sum = results.tile([P, SPLIT], F32, tag="last_sum_rows", name="last_sum_rows")
                nc.scalar.copy(out=last_sum[:], in_=last_sums[s][:])
                nc.sync.dma_start(out=out_0[:, pair * PAIR + s, :SPLIT], in_=last_sum[:])

        def pool(pair, s, cols):
            if pair > 0:
                nc.vector.tensor_tensor(
                    out=best[:, s, cols],
                    in0=best[:, s, cols],
                    in1=gated[pair][:, s, cols],
                    op=ALU.max,
                )

        pooled = consts.tile([P, OUTPUTS], F32, name="pooled")

        def join_slices(cols):
            nc.vector.tensor_tensor(
                out=pooled[:, cols], in0=best[:, 0, cols], in1=best[:, 1, cols], op=ALU.max
            )

        def add_bias_to_best_and_store(cols):
            nc.vector.tensor_tensor(
                out=pooled[:, cols], in0=pooled[:, cols], in1=gated_bias[:, cols], op=ALU.add
            )
            nc.sync.dma_start(out=out_1[:, cols], in_=pooled[:, cols])

        def step(n):
            if n == CONTEXT:
                open_gate()
            if n == PAIRS - 1:
                open_last_sums()
            if n >= 0:
                multiply(n)
            if n == 0:
                keep_gated_bias()
            if n == PAIRS - 1:
                close_last_sums_and_store(n)
            if size_of(n + 2) and by_vector(n + 2):
                measure(n + 2)
            elif size_of(n + 2):
                spread(n + 2, 1)
                take_root(n + 2)
            for s in range(PAIR):
                if s < size_of(n + 1):
                    activate(n + 1, s)
                if s < size_of(n + 3):
                    turn(n + 3, s)
            if size_of(n + 1):
                regroup_last_columns(n + 1)
            if size_of(n + 3) and not by_vector(n + 3):
                take_means(n + 3, 0)
                spread(n + 3, 0)
                take_means(n + 3, 1)
            if n == PAIRS - 1:
                return
            long_steps = []
            if n >= 0:
                bias_steps = add_bias_steps(n)
                gate_step = lambda: gate_next(n)
            if n == 0:
                long_steps += [gate_step, gate_step, bias_steps[0]]
            elif n > 0:
                long_steps += [bias_steps[0], gate_step, bias_steps[1]]
            before_regrouping = max(len(long_steps) - 1, 0)
            if size_of(n + 1) and scalar_columns(n + 1):
                long_steps.append(lambda: regroup_first_columns(n + 1))
            if n > 0:
                long_steps.append(gate_step)
            if size_of(n + 1):
                long_steps.append(lambda: quantise(n + 1))
            if n == 0:
                long_steps.append(bias_steps[1])
            elif n > 0:
                long_steps += [lambda s=s: pool(n, s, slice(0, OUTPUTS)) for s in range(PAIR)]
            short_steps = coefficient_steps(n + 2) if size_of(n + 2) else []
            for k in range(max(len(long_steps), before_regrouping + len(short_steps))):
                if k < len(long_steps):
                    long_steps[k]()
                if 0 <= k - before_regrouping < len(short_steps):
                    short_steps[k - before_regrouping]()
            if n > 0:
                add_first_columns_and_store(n)

        step(CONTEXT - 3)
        step(CONTEXT - 2)
        for half in range(HALVES):
            quantise_weight_half(c_w_rows, c_w_codes, c_w_planes, half)
        spread_context_bias()
        step(CONTEXT - 1)
        for half in range(HALVES):
            quantise_weight_half(s_w_rows, s_w_codes, s_w_planes, half)
        step(CONTEXT)
        with tc.manual_schedule():
            for n in range(PAIRS):
                step(n)
            last = PAIRS - 1
            first_half, last_half = (slice(h * N_TILE, (h + 1) * N_TILE) for h in range(HALVES))
            for s in range(PAIR):
                pool(last, s, first_half)
            for add_bias in add_bias_steps(last):
                add_bias()
            join_slices(first_half)
            for s in range(PAIR):
                pool(last, s, last_half)
            add_bias_to_best_and_store(first_half)
            join_slices(last_half)
            add_bias_to_best_and_store(last_half)
